import numpy as np
import ml_dtypes


def mxq(x, axis, fmt="e4m3"):
    dtype, down = {"e4m3": (ml_dtypes.float8_e4m3fn, 7), "e5m2": (ml_dtypes.float8_e5m2, 14)}[fmt]
    v = np.moveaxis(np.asarray(x, np.float32).astype(ml_dtypes.bfloat16).astype(np.float64), axis, -1)
    blocks = v.reshape(v.shape[:-1] + (-1, 32))
    amax = np.abs(blocks).max(-1, keepdims=True)
    byte = np.maximum(np.where(amax > 0, np.frexp(amax)[1] - 1 + 127, 0) - down, 1)
    scale = np.exp2(byte - 127.0)
    codes = (blocks / scale).astype(np.float32).astype(dtype).astype(np.float64)
    return np.moveaxis((codes * scale).reshape(v.shape), -1, axis)


WIDE = False


def mx_kscale(k):
    if not WIDE:
        return np.ones(k)
    levels = np.array([10, -10, 5, -5, 0])
    if k % 512:
        return np.exp2(np.random.permutation(np.resize(levels, k // 32))).repeat(32)
    a = np.empty((k // 512, 16))
    for p in range(k // 512):
        a[p, :8] = np.random.permutation(np.resize(levels, 8))
        for g in range(8):
            far = levels[np.abs(levels - a[p, g]) >= 10]
            a[p, g + 8] = far[np.random.randint(len(far))]
    return np.exp2(a.ravel()).repeat(32)


BF16 = ml_dtypes.bfloat16


def bf(x):
    return np.asarray(x, np.float32).astype(BF16)


def f64(x):
    return np.asarray(x).astype(np.float64)


B, R, C, H, DH = 64, 8, 1024, 4, 128
T = R * R
E = H * DH
EPS = 2.0 ** -23


def rmsnorm(v):
    return v * (1.0 / np.sqrt(np.mean(np.square(v), axis=-1, keepdims=True) + EPS))


def setup_inputs():
    s = mx_kscale(C)
    return {"x": bf(np.random.standard_normal((B, T, C)) * s),
            "Wq": bf(np.random.standard_normal((C, E)) / np.sqrt(C) / s[:, None]),
            "Wk": bf(np.random.standard_normal((C, E)) / np.sqrt(C) / s[:, None])}


def reference(x, Wq, Wk):
    xq = mxq(f64(x), 2, "e4m3")

    def proj(W):
        return (xq @ mxq(f64(W), 0, "e4m3")).reshape(B, T, H, DH).transpose(0, 2, 1, 3)

    return rmsnorm(proj(Wq)), rmsnorm(proj(Wk))

@@ -1,0 +1,271 @@
+from contextlib import ExitStack
+
+import concourse.mybir as mybir
+from concourse.masks import make_identity
+
+F32 = mybir.dt.float32
+BF16 = mybir.dt.bfloat16
+U32 = mybir.dt.uint32
+U8 = mybir.dt.uint8
+FP8X4 = mybir.dt.float8_e4m3fn_x4
+ACT = mybir.ActivationFunctionType
+ALU = mybir.AluOpType
+
+P = 128
+BOARDS, SQUARES, C = 64, 64, 1024
+H, DH = 4, 128
+E = H * DH
+EPS = 2.0**-23
+TOKENS = BOARDS * SQUARES
+
+PACK = 4
+K_PASS = P * PACK
+PASSES = C // K_PASS
+WORD_PLANES = 2
+
+GROUP_TILES = 8
+GROUP_TOKENS = P * GROUP_TILES
+GROUP_BOARDS = GROUP_TOKENS // SQUARES
+RUNS = SQUARES // GROUP_TILES
+BLOCK_TILES = 4
+PAIR = 2
+BLOCKS = TOKENS // (P * BLOCK_TILES)
+BLOCKS_IN_GROUP = GROUP_TILES // BLOCK_TILES
+PAIRS_IN_BLOCK = BLOCK_TILES // PAIR
+PAIRS = BLOCKS * PAIRS_IN_BLOCK
+UNITS_IN_BLOCK = 2 * PAIRS_IN_BLOCK
+UNITS = BLOCKS * UNITS_IN_BLOCK
+PAIRS_AHEAD = 2
+
+FLOPS = 2 * TOKENS * C * 2 * E
+
+
+def tile_pieceroutedattention_pa_t_kernel(tc, x, Wq, Wk, out_0, out_1):
+    nc = tc.nc
+    weights = (Wq, Wk)
+    x_tiles = x.flatten_outer_dims().rearrange("(g p i) c -> g p i c", p=P, i=GROUP_TILES)
+    out_runs = [
+        out.rearrange("b h (r i) d -> h b r (i d)", i=GROUP_TILES) for out in (out_0, out_1)
+    ]
+
+    with ExitStack() as stack:
+        stack.enter_context(tc.manual_schedule())
+        keep = stack.enter_context(tc.tile_pool(name="keep", bufs=1))
+        w_pool = stack.enter_context(tc.tile_pool(name="w", bufs=2))
+        x_pool = stack.enter_context(tc.tile_pool(name="x", bufs=BLOCKS))
+        stage = stack.enter_context(tc.tile_pool(name="stage", bufs=2))
+        codes_pool = stack.enter_context(tc.tile_pool(name="codes", bufs=2 * PAIRS_IN_BLOCK + 1))
+        small = stack.enter_context(tc.tile_pool(name="small", bufs=4))
+        res_pool = stack.enter_context(tc.tile_pool(name="res", bufs=6))
+        psum_x = stack.enter_context(tc.psum_pool(name="psum_x", bufs=PAIR))
+        psum_y = stack.enter_context(tc.psum_pool(name="psum_y", bufs=3 * PAIR))
+
+        w_raw = {}
+        w_grouped = {}
+        x_blocks = {}
+        turned = {}
+        grouped = {}
+        quantised = {}
+        sums = {}
+        sum_sq = {}
+        inv_rms = {}
+        results = {}
+
+        def load_weight(half):
+            raw = w_pool.tile([P, PASSES, PACK, E], BF16)
+            for g in range(PASSES):
+                nc.sync.dma_start(
+                    out=raw[:, g, :, :],
+                    in_=weights[half][g * K_PASS : (g + 1) * K_PASS, :].rearrange(
+                        "(p t) n -> p t n", t=PACK
+                    ),
+                )
+            w_raw[half] = raw
+
+        def load_tokens(blk):
+            grp, first = divmod(blk * BLOCK_TILES, GROUP_TILES)
+            x_sb = x_pool.tile([P, BLOCK_TILES, C], BF16)
+            for pr in range(PAIRS_IN_BLOCK):
+                nc.sync.dma_start(
+                    out=x_sb[:, pr * PAIR : (pr + 1) * PAIR, :],
+                    in_=x_tiles[grp, :, first + pr * PAIR : first + (pr + 1) * PAIR, :],
+                )
+            x_blocks[blk] = x_sb
+
+        def regroup_weight(half, g):
+            side_by_side = w_pool.tile([P, E, PACK], BF16, align_bytes=64)
+            nc.vector.tensor_copy(
+                out=side_by_side[:].rearrange("p (c i) t -> p c t i", i=4),
+                in_=w_raw[half][:, g, :, :].rearrange("p t (c i) -> p c t i", i=4),
+            )
+            w_grouped[(half, g)] = side_by_side
+
+        def quantise_weight(half, g):
+            nc.vector.quantize_mx(
+                out=w_codes[:, g, half, :].bitcast(FP8X4),
+                scales=w_scales[:, g, half, :],
+                in_=w_grouped[(half, g)][:].rearrange("p n t -> p (n t)"),
+            )
+
+        def turn(pair):
+            blk, pr = divmod(pair, PAIRS_IN_BLOCK)
+            banks = []
+            for j in range(PAIR):
+                words = x_blocks[blk][:, pr * PAIR + j, :].bitcast(F32)
+                bank = psum_x.tile([P, PASSES * WORD_PLANES, P], F32)
+                for c in range(PASSES * WORD_PLANES):
+                    g, u = divmod(c, WORD_PLANES)
+                    first = g * WORD_PLANES * P + u
+                    nc.tensor.transpose(
+                        bank[:, c, :],
+                        words[:, first : (g + 1) * WORD_PLANES * P : WORD_PLANES],
+                        ident[:],
+                    )
+                banks.append(bank)
+            turned[pair] = banks
+            side_by_side = stage.tile([P, PAIR, PASSES, P, PACK], BF16, align_bytes=64)
+            grouped[pair] = side_by_side
+
+        def regroup_tokens(pair, j, copy):
+            copy(
+                out=grouped[pair][:, j]
+                .rearrange("p g r t -> p (g r t)")
+                .bitcast(F32)
+                .rearrange("p (g r u) -> p g r u", g=PASSES, u=WORD_PLANES),
+                in_=turned[pair][j][:].rearrange("p (g u) r -> p g r u", u=WORD_PLANES),
+            )
+
+        def quantise_tokens(pair):
+            x_codes = codes_pool.tile([P, PAIR, PASSES, P], U32, align_bytes=64)
+            x_scales = codes_pool.tile([P, PAIR, PASSES, P], U8, align_bytes=64)
+            nc.vector.quantize_mx(
+                out=x_codes[:].rearrange("p j g r -> p (j g r)").bitcast(FP8X4),
+                scales=x_scales[:].rearrange("p j g r -> p (j g r)"),
+                in_=grouped[pair][:].rearrange("p j g r t -> p (j g r t)"),
+            )
+            quantised[pair] = (x_codes, x_scales)
+
+        def place(unit):
+            blk, rest = divmod(unit, UNITS_IN_BLOCK)
+            half, pr = divmod(rest, PAIRS_IN_BLOCK)
+            return blk, half, pr
+
+        def project(unit):
+            blk, half, pr = place(unit)
+            x_codes, x_scales = quantised[blk * PAIRS_IN_BLOCK + pr]
+            banks = []
+            for j in range(PAIR):
+                y = psum_y.tile([P, E], F32)
+                for g in range(PASSES):
+                    nc.tensor.matmul_mx(
+                        out=y[:],
+                        lhsT=x_codes[:, j, g, :].bitcast(FP8X4),
+                        lhsT_scale=x_scales[:, j, g, :],
+                        rhs=w_codes[:, g, half, :].bitcast(FP8X4),
+                        rhs_scale=w_scales[:, g, half, :],
+                        start=(g == 0),
+                        stop=(g == PASSES - 1),
+                    )
+                banks.append(y)
+            sums[unit] = banks
+            totals = small.tile([P, PAIR, H], F32)
+            sum_sq[unit] = totals
+
+        def sum_squares(unit, j):
+            squares = small.tile([P, H, DH], BF16)
+            for h in range(H):
+                nc.scalar.activation(
+                    out=squares[:, h, :],
+                    in_=sums[unit][j][:, h * DH : (h + 1) * DH],
+                    func=ACT.Square,
+                    accum_out=sum_sq[unit][:, j, h : h + 1],
+                )
+
+        def inverse_rms(unit):
+            factors = small.tile([P, PAIR, H], F32)
+            nc.scalar.activation(
+                out=factors[:],
+                in_=sum_sq[unit][:],
+                func=ACT.Abs_reciprocal_sqrt,
+                scale=1.0 / DH,
+                bias=eps[:, 0:1],
+            )
+            inv_rms[unit] = factors
+
+        def normalise(unit):
+            blk, half, pr = place(unit)
+            if pr == 0:
+                res = res_pool.tile([P, H, BLOCK_TILES, DH], F32)
+                results[(blk, half)] = res
+            res = results[(blk, half)]
+            for j in range(PAIR):
+                nc.vector.tensor_tensor(
+                    out=res[:, :, pr * PAIR + j, :],
+                    in0=sums[unit][j][:].rearrange("p (h d) -> p h d", h=H),
+                    in1=inv_rms[unit][:, j, :].unsqueeze(2).to_broadcast([P, H, DH]),
+                    op=ALU.mult,
+                )
+            if pr == PAIRS_IN_BLOCK - 1:
+                grp, part = divmod(blk, BLOCKS_IN_GROUP)
+                run = BLOCK_TILES * DH
+                for h in range(H):
+                    nc.sync.dma_start(
+                        out=out_runs[half][
+                            h,
+                            grp * GROUP_BOARDS : (grp + 1) * GROUP_BOARDS,
+                            :,
+                            part * run : (part + 1) * run,
+                        ],
+                        in_=res[:, h, :, :].rearrange("p i d -> p (i d)"),
+                    )
+
+        load_weight(0)
+        load_tokens(0)
+        load_weight(1)
+        for blk in range(1, BLOCKS):
+            load_tokens(blk)
+
+        ident = keep.tile([P, P], F32)
+        make_identity(nc, ident[:])
+        eps = keep.tile([P, 1], F32)
+        nc.vector.memset(eps[:], EPS)
+        warm = keep.tile([P, 1], F32)
+        nc.scalar.activation(out=warm[:], in_=eps[:], func=ACT.Abs_reciprocal_sqrt)
+        w_codes = keep.tile([P, PASSES, 2, E], U32, align_bytes=64)
+        w_scales = keep.tile([P, PASSES, 2, E], U8, align_bytes=64)
+
+        for g in range(PASSES):
+            regroup_weight(0, g)
+        for g in range(PASSES):
+            quantise_weight(0, g)
+        for pair in range(PAIRS_AHEAD):
+            turn(pair)
+            for j in range(PAIR):
+                regroup_tokens(pair, j, nc.scalar.copy)
+        quantise_tokens(0)
+        regroup_weight(1, 0)
+        quantise_tokens(1)
+        regroup_weight(1, 1)
+        for g in range(PASSES):
+            quantise_weight(1, g)
+
+        for u in range(UNITS + 1):
+            ahead = u // 2 + PAIRS_AHEAD
+            prepare = u % 2 == 0 and ahead < PAIRS
+            if u < UNITS:
+                project(u)
+            if prepare:
+                turn(ahead)
+            if u < UNITS:
+                sum_squares(u, 0)
+            if u > 0:
+                inverse_rms(u - 1)
+            if prepare:
+                regroup_tokens(ahead, 0, nc.scalar.copy)
+                regroup_tokens(ahead, 1, nc.vector.tensor_copy)
+            if u < UNITS:
+                sum_squares(u, 1)
+            if u > 0:
+                normalise(u - 1)
+            if prepare:
+                quantise_tokens(ahead)

@@ -23,7 +23,7 @@ K_PASS = P * PACK
 PASSES = C // K_PASS
 WORD_PLANES = 2
 
-GROUP_TILES = 8
+GROUP_TILES = 32
 GROUP_TOKENS = P * GROUP_TILES
 GROUP_BOARDS = GROUP_TOKENS // SQUARES
 RUNS = SQUARES // GROUP_TILES

@@ -52,7 +52,7 @@ def tile_pieceroutedattention_pa_t_kernel(tc, x, Wq, Wk, out_0, out_1):
         stack.enter_context(tc.manual_schedule())
         keep = stack.enter_context(tc.tile_pool(name="keep", bufs=1))
         w_pool = stack.enter_context(tc.tile_pool(name="w", bufs=2))
-        x_pool = stack.enter_context(tc.tile_pool(name="x", bufs=BLOCKS))
+        x_pool = stack.enter_context(tc.tile_pool(name="x", bufs=PAIRS))
         stage = stack.enter_context(tc.tile_pool(name="stage", bufs=2))
         codes_pool = stack.enter_context(tc.tile_pool(name="codes", bufs=2 * PAIRS_IN_BLOCK + 1))
         small = stack.enter_context(tc.tile_pool(name="small", bufs=4))
@@ -62,7 +62,7 @@ def tile_pieceroutedattention_pa_t_kernel(tc, x, Wq, Wk, out_0, out_1):
 
         w_raw = {}
         w_grouped = {}
-        x_blocks = {}
+        x_pairs = {}
         turned = {}
         grouped = {}
         quantised = {}
@@ -82,22 +82,24 @@ def tile_pieceroutedattention_pa_t_kernel(tc, x, Wq, Wk, out_0, out_1):
                 )
             w_raw[half] = raw
 
-        def load_tokens(blk):
-            grp, first = divmod(blk * BLOCK_TILES, GROUP_TILES)
-            x_sb = x_pool.tile([P, BLOCK_TILES, C], BF16)
-            for pr in range(PAIRS_IN_BLOCK):
+        def load_tokens(pair, dmas):
+            grp, first = divmod(pair * PAIR, GROUP_TILES)
+            x_sb = x_pool.tile([P, PAIR, C], BF16)
+            step = PAIR // dmas
+            for j in range(0, PAIR, step):
                 nc.sync.dma_start(
-                    out=x_sb[:, pr * PAIR : (pr + 1) * PAIR, :],
-                    in_=x_tiles[grp, :, first + pr * PAIR : first + (pr + 1) * PAIR, :],
+                    out=x_sb[:, j : j + step, :],
+                    in_=x_tiles[grp, :, first + j : first + j + step, :],
                 )
-            x_blocks[blk] = x_sb
+            x_pairs[pair] = x_sb
 
-        def regroup_weight(half, g):
+        def regroup_weight(half, g, shares):
             side_by_side = w_pool.tile([P, E, PACK], BF16, align_bytes=64)
-            nc.vector.tensor_copy(
-                out=side_by_side[:].rearrange("p (c i) t -> p c t i", i=4),
-                in_=w_raw[half][:, g, :, :].rearrange("p t (c i) -> p c t i", i=4),
-            )
+            for copy, first, end in shares:
+                copy(
+                    out=side_by_side[:, first:end, :].rearrange("p (c i) t -> p c t i", i=4),
+                    in_=w_raw[half][:, g, :, first:end].rearrange("p t (c i) -> p c t i", i=4),
+                )
             w_grouped[(half, g)] = side_by_side
 
         def quantise_weight(half, g):
@@ -108,10 +110,9 @@ def tile_pieceroutedattention_pa_t_kernel(tc, x, Wq, Wk, out_0, out_1):
             )
 
         def turn(pair):
-            blk, pr = divmod(pair, PAIRS_IN_BLOCK)
             banks = []
             for j in range(PAIR):
-                words = x_blocks[blk][:, pr * PAIR + j, :].bitcast(F32)
+                words = x_pairs[pair][:, j, :].bitcast(F32)
                 bank = psum_x.tile([P, PASSES * WORD_PLANES, P], F32)
                 for c in range(PASSES * WORD_PLANES):
                     g, u = divmod(c, WORD_PLANES)
@@ -150,23 +151,23 @@ def tile_pieceroutedattention_pa_t_kernel(tc, x, Wq, Wk, out_0, out_1):
             half, pr = divmod(rest, PAIRS_IN_BLOCK)
             return blk, half, pr
 
-        def project(unit):
+        def project(unit, order):
             blk, half, pr = place(unit)
             x_codes, x_scales = quantised[blk * PAIRS_IN_BLOCK + pr]
             banks = []
             for j in range(PAIR):
                 y = psum_y.tile([P, E], F32)
-                for g in range(PASSES):
-                    nc.tensor.matmul_mx(
-                        out=y[:],
-                        lhsT=x_codes[:, j, g, :].bitcast(FP8X4),
-                        lhsT_scale=x_scales[:, j, g, :],
-                        rhs=w_codes[:, g, half, :].bitcast(FP8X4),
-                        rhs_scale=w_scales[:, g, half, :],
-                        start=(g == 0),
-                        stop=(g == PASSES - 1),
-                    )
                 banks.append(y)
+            for j, g in order:
+                nc.tensor.matmul_mx(
+                    out=banks[j][:],
+                    lhsT=x_codes[:, j, g, :].bitcast(FP8X4),
+                    lhsT_scale=x_scales[:, j, g, :],
+                    rhs=w_codes[:, g, half, :].bitcast(FP8X4),
+                    rhs_scale=w_scales[:, g, half, :],
+                    start=(g == 0),
+                    stop=(g == PASSES - 1),
+                )
             sums[unit] = banks
             totals = small.tile([P, PAIR, H], F32)
             sum_sq[unit] = totals
@@ -205,25 +206,28 @@ def tile_pieceroutedattention_pa_t_kernel(tc, x, Wq, Wk, out_0, out_1):
                     in1=inv_rms[unit][:, j, :].unsqueeze(2).to_broadcast([P, H, DH]),
                     op=ALU.mult,
                 )
-            if pr == PAIRS_IN_BLOCK - 1:
+            last = blk == BLOCKS - 1
+            if last or pr == PAIRS_IN_BLOCK - 1:
                 grp, part = divmod(blk, BLOCKS_IN_GROUP)
-                run = BLOCK_TILES * DH
+                first = pr * PAIR if last else 0
+                end = (pr + 1) * PAIR
                 for h in range(H):
                     nc.sync.dma_start(
                         out=out_runs[half][
                             h,
                             grp * GROUP_BOARDS : (grp + 1) * GROUP_BOARDS,
                             :,
-                            part * run : (part + 1) * run,
+                            (part * BLOCK_TILES + first) * DH : (part * BLOCK_TILES + end) * DH,
                         ],
-                        in_=res[:, h, :, :].rearrange("p i d -> p (i d)"),
+                        in_=res[:, h, first:end, :].rearrange("p i d -> p (i d)"),
                     )
 
+        load_tokens(0, 2)
         load_weight(0)
-        load_tokens(0)
+        load_tokens(1, 1)
         load_weight(1)
-        for blk in range(1, BLOCKS):
-            load_tokens(blk)
+        for pair in range(2, PAIRS):
+            load_tokens(pair, 1)
 
         ident = keep.tile([P, P], F32)
         make_identity(nc, ident[:])
@@ -234,38 +238,55 @@ def tile_pieceroutedattention_pa_t_kernel(tc, x, Wq, Wk, out_0, out_1):
         w_codes = keep.tile([P, PASSES, 2, E], U32, align_bytes=64)
         w_scales = keep.tile([P, PASSES, 2, E], U8, align_bytes=64)
 
-        for g in range(PASSES):
-            regroup_weight(0, g)
+        TILE_BY_TILE = [(j, g) for j in range(PAIR) for g in range(PASSES)]
+        PASS_BY_PASS = [(j, g) for g in range(PASSES) for j in range(PAIR)]
+        VECTOR_ALONE = [(nc.vector.tensor_copy, 0, E)]
+        SHARED = [(nc.scalar.copy, E // 2, E), (nc.vector.tensor_copy, 0, E // 2)]
+
+        turn(0)
+        for j in range(PAIR):
+            regroup_tokens(0, j, nc.scalar.copy)
+        regroup_weight(0, 0, VECTOR_ALONE)
+        quantise_tokens(0)
+        regroup_weight(0, 1, SHARED)
         for g in range(PASSES):
             quantise_weight(0, g)
-        for pair in range(PAIRS_AHEAD):
-            turn(pair)
-            for j in range(PAIR):
-                regroup_tokens(pair, j, nc.scalar.copy)
-        quantise_tokens(0)
-        regroup_weight(1, 0)
+        turn(1)
+        for j in range(PAIR):
+            regroup_tokens(1, j, nc.scalar.copy)
+        project(0, PASS_BY_PASS)
         quantise_tokens(1)
-        regroup_weight(1, 1)
+        project(1, TILE_BY_TILE)
+        for g in range(PASSES):
+            regroup_weight(1, g, VECTOR_ALONE)
         for g in range(PASSES):
             quantise_weight(1, g)
+        sum_squares(0, 0)
+        sum_squares(0, 1)
+        turn(2)
+        sum_squares(1, 0)
+        inverse_rms(0)
+        for j in range(PAIR):
+            regroup_tokens(2, j, nc.scalar.copy)
+        sum_squares(1, 1)
+        normalise(0)
+        quantise_tokens(2)
 
-        for u in range(UNITS + 1):
+        for u in range(2, UNITS + 1):
             ahead = u // 2 + PAIRS_AHEAD
             prepare = u % 2 == 0 and ahead < PAIRS
             if u < UNITS:
-                project(u)
+                project(u, TILE_BY_TILE)
             if prepare:
                 turn(ahead)
             if u < UNITS:
                 sum_squares(u, 0)
-            if u > 0:
-                inverse_rms(u - 1)
+            inverse_rms(u - 1)
             if prepare:
                 regroup_tokens(ahead, 0, nc.scalar.copy)
                 regroup_tokens(ahead, 1, nc.vector.tensor_copy)
             if u < UNITS:
                 sum_squares(u, 1)
-            if u > 0:
-                normalise(u - 1)
+            normalise(u - 1)
             if prepare:
                 quantise_tokens(ahead)

@@ -52,11 +52,11 @@ def tile_pieceroutedattention_pa_t_kernel(tc, x, Wq, Wk, out_0, out_1):
         stack.enter_context(tc.manual_schedule())
         keep = stack.enter_context(tc.tile_pool(name="keep", bufs=1))
         w_pool = stack.enter_context(tc.tile_pool(name="w", bufs=2))
+        large_pool = stack.enter_context(tc.tile_pool(name="large", bufs=2 * BLOCKS))
         x_pool = stack.enter_context(tc.tile_pool(name="x", bufs=PAIRS))
         stage = stack.enter_context(tc.tile_pool(name="stage", bufs=2))
         codes_pool = stack.enter_context(tc.tile_pool(name="codes", bufs=2 * PAIRS_IN_BLOCK + 1))
         small = stack.enter_context(tc.tile_pool(name="small", bufs=4))
-        res_pool = stack.enter_context(tc.tile_pool(name="res", bufs=6))
         psum_x = stack.enter_context(tc.psum_pool(name="psum_x", bufs=PAIR))
         psum_y = stack.enter_context(tc.psum_pool(name="psum_y", bufs=3 * PAIR))
 
@@ -72,7 +72,7 @@ def tile_pieceroutedattention_pa_t_kernel(tc, x, Wq, Wk, out_0, out_1):
         results = {}
 
         def load_weight(half):
-            raw = w_pool.tile([P, PASSES, PACK, E], BF16)
+            raw = large_pool.tile([P, PASSES, PACK, E], BF16, tag="large")
             for g in range(PASSES):
                 nc.sync.dma_start(
                     out=raw[:, g, :, :],
@@ -182,30 +182,32 @@ def tile_pieceroutedattention_pa_t_kernel(tc, x, Wq, Wk, out_0, out_1):
                     accum_out=sum_sq[unit][:, j, h : h + 1],
                 )
 
-        def inverse_rms(unit):
+        def inverse_rms(unit, first, end):
             factors = small.tile([P, PAIR, H], F32)
             nc.scalar.activation(
-                out=factors[:],
-                in_=sum_sq[unit][:],
+                out=factors[:, first:end, :],
+                in_=sum_sq[unit][:, first:end, :],
                 func=ACT.Abs_reciprocal_sqrt,
                 scale=1.0 / DH,
                 bias=eps[:, 0:1],
             )
-            inv_rms[unit] = factors
+            for j in range(first, end):
+                inv_rms[(unit, j)] = factors
 
-        def normalise(unit):
+        def normalise(unit, j):
             blk, half, pr = place(unit)
-            if pr == 0:
-                res = res_pool.tile([P, H, BLOCK_TILES, DH], F32)
+            if pr == 0 and j == 0:
+                res = large_pool.tile([P, H, BLOCK_TILES, DH], F32, tag="large")
                 results[(blk, half)] = res
-            res = results[(blk, half)]
-            for j in range(PAIR):
-                nc.vector.tensor_tensor(
-                    out=res[:, :, pr * PAIR + j, :],
-                    in0=sums[unit][j][:].rearrange("p (h d) -> p h d", h=H),
-                    in1=inv_rms[unit][:, j, :].unsqueeze(2).to_broadcast([P, H, DH]),
-                    op=ALU.mult,
-                )
+            nc.vector.tensor_tensor(
+                out=results[(blk, half)][:, :, pr * PAIR + j, :],
+                in0=sums[unit][j][:].rearrange("p (h d) -> p h d", h=H),
+                in1=inv_rms[(unit, j)][:, j, :].unsqueeze(2).to_broadcast([P, H, DH]),
+                op=ALU.mult,
+            )
+
+        def store(unit):
+            blk, half, pr = place(unit)
             last = blk == BLOCKS - 1
             if last or pr == PAIRS_IN_BLOCK - 1:
                 grp, part = divmod(blk, BLOCKS_IN_GROUP)
@@ -219,7 +221,7 @@ def tile_pieceroutedattention_pa_t_kernel(tc, x, Wq, Wk, out_0, out_1):
                             :,
                             (part * BLOCK_TILES + first) * DH : (part * BLOCK_TILES + end) * DH,
                         ],
-                        in_=res[:, h, first:end, :].rearrange("p i d -> p (i d)"),
+                        in_=results[(blk, half)][:, h, first:end, :].rearrange("p i d -> p (i d)"),
                     )
 
         load_tokens(0, 2)
@@ -246,7 +248,7 @@ def tile_pieceroutedattention_pa_t_kernel(tc, x, Wq, Wk, out_0, out_1):
         turn(0)
         for j in range(PAIR):
             regroup_tokens(0, j, nc.scalar.copy)
-        regroup_weight(0, 0, VECTOR_ALONE)
+        regroup_weight(0, 0, SHARED)
         quantise_tokens(0)
         regroup_weight(0, 1, SHARED)
         for g in range(PASSES):
@@ -255,38 +257,46 @@ def tile_pieceroutedattention_pa_t_kernel(tc, x, Wq, Wk, out_0, out_1):
         for j in range(PAIR):
             regroup_tokens(1, j, nc.scalar.copy)
         project(0, PASS_BY_PASS)
+        regroup_weight(1, 0, VECTOR_ALONE)
         quantise_tokens(1)
         project(1, TILE_BY_TILE)
-        for g in range(PASSES):
-            regroup_weight(1, g, VECTOR_ALONE)
+        regroup_weight(1, 1, VECTOR_ALONE)
         for g in range(PASSES):
             quantise_weight(1, g)
         sum_squares(0, 0)
         sum_squares(0, 1)
         turn(2)
         sum_squares(1, 0)
-        inverse_rms(0)
+        inverse_rms(0, 0, PAIR)
         for j in range(PAIR):
             regroup_tokens(2, j, nc.scalar.copy)
         sum_squares(1, 1)
-        normalise(0)
+        for j in range(PAIR):
+            normalise(0, j)
         quantise_tokens(2)
 
-        for u in range(2, UNITS + 1):
+        for u in range(2, UNITS):
+            even = u % 2 == 0
             ahead = u // 2 + PAIRS_AHEAD
-            prepare = u % 2 == 0 and ahead < PAIRS
-            if u < UNITS:
-                project(u, TILE_BY_TILE)
-            if prepare:
+            prepare = ahead < PAIRS
+            project(u, TILE_BY_TILE)
+            if even and prepare:
                 turn(ahead)
-            if u < UNITS:
-                sum_squares(u, 0)
-            inverse_rms(u - 1)
-            if prepare:
+            sum_squares(u, 0)
+            inverse_rms(u - 1, 0, PAIR)
+            if u == UNITS - 1:
+                inverse_rms(u, 0, 1)
+            sum_squares(u, 1)
+            if even and prepare:
                 regroup_tokens(ahead, 0, nc.scalar.copy)
+            normalise(u - 1, 0)
+            if prepare and even:
                 regroup_tokens(ahead, 1, nc.vector.tensor_copy)
-            if u < UNITS:
-                sum_squares(u, 1)
-            normalise(u - 1)
-            if prepare:
+            if prepare and not even:
                 quantise_tokens(ahead)
+            normalise(u - 1, 1)
+            store(u - 1)
+        normalise(UNITS - 1, 0)
+        inverse_rms(UNITS - 1, 1, PAIR)
+        normalise(UNITS - 1, 1)
+        store(UNITS - 1)

@@ -45,7 +45,7 @@ def tile_pieceroutedattention_pa_t_kernel(tc, x, Wq, Wk, out_0, out_1):
     weights = (Wq, Wk)
     x_tiles = x.flatten_outer_dims().rearrange("(g p i) c -> g p i c", p=P, i=GROUP_TILES)
     out_runs = [
-        out.rearrange("b h (r i) d -> h b r (i d)", i=GROUP_TILES) for out in (out_0, out_1)
+        out.rearrange("b h (r i) d -> r b h (i d)", i=GROUP_TILES) for out in (out_0, out_1)
     ]
 
     with ExitStack() as stack:
@@ -53,7 +53,7 @@ def tile_pieceroutedattention_pa_t_kernel(tc, x, Wq, Wk, out_0, out_1):
         keep = stack.enter_context(tc.tile_pool(name="keep", bufs=1))
         w_pool = stack.enter_context(tc.tile_pool(name="w", bufs=2))
         large_pool = stack.enter_context(tc.tile_pool(name="large", bufs=2 * BLOCKS))
-        x_pool = stack.enter_context(tc.tile_pool(name="x", bufs=PAIRS))
+        x_pool = stack.enter_context(tc.tile_pool(name="x", bufs=BLOCKS))
         stage = stack.enter_context(tc.tile_pool(name="stage", bufs=2))
         codes_pool = stack.enter_context(tc.tile_pool(name="codes", bufs=2 * PAIRS_IN_BLOCK + 1))
         small = stack.enter_context(tc.tile_pool(name="small", bufs=4))
@@ -62,7 +62,7 @@ def tile_pieceroutedattention_pa_t_kernel(tc, x, Wq, Wk, out_0, out_1):
 
         w_raw = {}
         w_grouped = {}
-        x_pairs = {}
+        x_blocks = {}
         turned = {}
         grouped = {}
         quantised = {}
@@ -82,16 +82,15 @@ def tile_pieceroutedattention_pa_t_kernel(tc, x, Wq, Wk, out_0, out_1):
                 )
             w_raw[half] = raw
 
-        def load_tokens(pair, dmas):
-            grp, first = divmod(pair * PAIR, GROUP_TILES)
-            x_sb = x_pool.tile([P, PAIR, C], BF16)
-            step = PAIR // dmas
-            for j in range(0, PAIR, step):
-                nc.sync.dma_start(
-                    out=x_sb[:, j : j + step, :],
-                    in_=x_tiles[grp, :, first + j : first + j + step, :],
-                )
-            x_pairs[pair] = x_sb
+        def load_tokens(blk, first, end):
+            if first == 0:
+                x_sb = x_pool.tile([P, BLOCK_TILES, C], BF16)
+                x_blocks[blk] = x_sb
+            grp, start = divmod(blk * BLOCK_TILES, GROUP_TILES)
+            nc.sync.dma_start(
+                out=x_blocks[blk][:, first:end, :],
+                in_=x_tiles[grp, :, start + first : start + end, :],
+            )
 
         def regroup_weight(half, g, shares):
             side_by_side = w_pool.tile([P, E, PACK], BF16, align_bytes=64)
@@ -110,9 +109,10 @@ def tile_pieceroutedattention_pa_t_kernel(tc, x, Wq, Wk, out_0, out_1):
             )
 
         def turn(pair):
+            blk, pr = divmod(pair, PAIRS_IN_BLOCK)
             banks = []
             for j in range(PAIR):
-                words = x_pairs[pair][:, j, :].bitcast(F32)
+                words = x_blocks[blk][:, pr * PAIR + j, :].bitcast(F32)
                 bank = psum_x.tile([P, PASSES * WORD_PLANES, P], F32)
                 for c in range(PASSES * WORD_PLANES):
                     g, u = divmod(c, WORD_PLANES)
@@ -208,28 +208,28 @@ def tile_pieceroutedattention_pa_t_kernel(tc, x, Wq, Wk, out_0, out_1):
 
         def store(unit):
             blk, half, pr = place(unit)
-            last = blk == BLOCKS - 1
-            if last or pr == PAIRS_IN_BLOCK - 1:
-                grp, part = divmod(blk, BLOCKS_IN_GROUP)
-                first = pr * PAIR if last else 0
+            by_pair = blk >= BLOCKS - 2
+            if by_pair or pr == PAIRS_IN_BLOCK - 1:
+                first = pr * PAIR if by_pair else 0
                 end = (pr + 1) * PAIR
-                for h in range(H):
+                start = blk * BLOCK_TILES
+                for r in range(RUNS):
                     nc.sync.dma_start(
-                        out=out_runs[half][
-                            h,
-                            grp * GROUP_BOARDS : (grp + 1) * GROUP_BOARDS,
-                            :,
-                            (part * BLOCK_TILES + first) * DH : (part * BLOCK_TILES + end) * DH,
-                        ],
-                        in_=results[(blk, half)][:, h, first:end, :].rearrange("p i d -> p (i d)"),
+                        out=out_runs[half][r, :, :, (start + first) * DH : (start + end) * DH],
+                        in_=results[(blk, half)][r:P:RUNS, :, first:end, :].rearrange(
+                            "p h i d -> p h (i d)"
+                        ),
                     )
 
-        load_tokens(0, 2)
+        load_tokens(0, 0, 1)
+        load_tokens(0, 1, PAIR)
         load_weight(0)
-        load_tokens(1, 1)
+        load_tokens(0, PAIR, BLOCK_TILES)
         load_weight(1)
-        for pair in range(2, PAIRS):
-            load_tokens(pair, 1)
+        load_tokens(1, 0, PAIR)
+        load_tokens(1, PAIR, BLOCK_TILES)
+        for blk in range(2, BLOCKS):
+            load_tokens(blk, 0, BLOCK_TILES)
 
         ident = keep.tile([P, P], F32)
         make_identity(nc, ident[:])

@@ -268,11 +268,11 @@ def tile_pieceroutedattention_pa_t_kernel(tc, x, Wq, Wk, out_0, out_1):
         turn(2)
         sum_squares(1, 0)
         inverse_rms(0, 0, PAIR)
-        for j in range(PAIR):
-            regroup_tokens(2, j, nc.scalar.copy)
         sum_squares(1, 1)
-        for j in range(PAIR):
-            normalise(0, j)
+        regroup_tokens(2, 0, nc.scalar.copy)
+        normalise(0, 0)
+        regroup_tokens(2, 1, nc.vector.tensor_copy)
+        normalise(0, 1)
         quantise_tokens(2)
 
         for u in range(2, UNITS):
@@ -289,11 +289,11 @@ def tile_pieceroutedattention_pa_t_kernel(tc, x, Wq, Wk, out_0, out_1):
             sum_squares(u, 1)
             if even and prepare:
                 regroup_tokens(ahead, 0, nc.scalar.copy)
+            if prepare and not even:
+                quantise_tokens(ahead)
             normalise(u - 1, 0)
             if prepare and even:
                 regroup_tokens(ahead, 1, nc.vector.tensor_copy)
-            if prepare and not even:
-                quantise_tokens(ahead)
             normalise(u - 1, 1)
             store(u - 1)
         normalise(UNITS - 1, 0)

@@ -148,7 +148,10 @@ def tile_pieceroutedattention_pa_t_kernel(tc, x, Wq, Wk, out_0, out_1):
 
         def place(unit):
             blk, rest = divmod(unit, UNITS_IN_BLOCK)
-            half, pr = divmod(rest, PAIRS_IN_BLOCK)
+            if blk == BLOCKS - 1:
+                pr, half = divmod(rest, 2)
+            else:
+                half, pr = divmod(rest, PAIRS_IN_BLOCK)
             return blk, half, pr
 
         def project(unit, order):
@@ -243,6 +246,7 @@ def tile_pieceroutedattention_pa_t_kernel(tc, x, Wq, Wk, out_0, out_1):
         TILE_BY_TILE = [(j, g) for j in range(PAIR) for g in range(PASSES)]
         PASS_BY_PASS = [(j, g) for g in range(PASSES) for j in range(PAIR)]
         VECTOR_ALONE = [(nc.vector.tensor_copy, 0, E)]
+        MOSTLY_VECTOR = [(nc.scalar.copy, 3 * E // 4, E), (nc.vector.tensor_copy, 0, 3 * E // 4)]
         SHARED = [(nc.scalar.copy, E // 2, E), (nc.vector.tensor_copy, 0, E // 2)]
 
         turn(0)
@@ -257,7 +261,7 @@ def tile_pieceroutedattention_pa_t_kernel(tc, x, Wq, Wk, out_0, out_1):
         for j in range(PAIR):
             regroup_tokens(1, j, nc.scalar.copy)
         project(0, PASS_BY_PASS)
-        regroup_weight(1, 0, VECTOR_ALONE)
+        regroup_weight(1, 0, MOSTLY_VECTOR)
         quantise_tokens(1)
         project(1, TILE_BY_TILE)
         regroup_weight(1, 1, VECTOR_ALONE)
@@ -289,12 +293,12 @@ def tile_pieceroutedattention_pa_t_kernel(tc, x, Wq, Wk, out_0, out_1):
             sum_squares(u, 1)
             if even and prepare:
                 regroup_tokens(ahead, 0, nc.scalar.copy)
+            normalise(u - 1, 0)
             if prepare and not even:
                 quantise_tokens(ahead)
-            normalise(u - 1, 0)
+            normalise(u - 1, 1)
             if prepare and even:
                 regroup_tokens(ahead, 1, nc.vector.tensor_copy)
-            normalise(u - 1, 1)
             store(u - 1)
         normalise(UNITS - 1, 0)
         inverse_rms(UNITS - 1, 1, PAIR)

from contextlib import ExitStack

import concourse.mybir as mybir
from concourse.masks import make_identity

F32 = mybir.dt.float32
BF16 = mybir.dt.bfloat16
U32 = mybir.dt.uint32
U8 = mybir.dt.uint8
FP8X4 = mybir.dt.float8_e4m3fn_x4
ACT = mybir.ActivationFunctionType
ALU = mybir.AluOpType

P = 128
BOARDS, SQUARES, C = 64, 64, 1024
H, DH = 4, 128
E = H * DH
EPS = 2.0**-23
TOKENS = BOARDS * SQUARES

PACK = 4
K_PASS = P * PACK
PASSES = C // K_PASS
WORD_PLANES = 2

GROUP_TILES = 32
GROUP_TOKENS = P * GROUP_TILES
GROUP_BOARDS = GROUP_TOKENS // SQUARES
RUNS = SQUARES // GROUP_TILES
BLOCK_TILES = 4
PAIR = 2
BLOCKS = TOKENS // (P * BLOCK_TILES)
BLOCKS_IN_GROUP = GROUP_TILES // BLOCK_TILES
PAIRS_IN_BLOCK = BLOCK_TILES // PAIR
PAIRS = BLOCKS * PAIRS_IN_BLOCK
UNITS_IN_BLOCK = 2 * PAIRS_IN_BLOCK
UNITS = BLOCKS * UNITS_IN_BLOCK
PAIRS_AHEAD = 2

FLOPS = 2 * TOKENS * C * 2 * E


def tile_pieceroutedattention_pa_t_kernel(tc, x, Wq, Wk, out_0, out_1):
    nc = tc.nc
    weights = (Wq, Wk)
    x_tiles = x.flatten_outer_dims().rearrange("(g p i) c -> g p i c", p=P, i=GROUP_TILES)
    out_runs = [
        out.rearrange("b h (r i) d -> r b h (i d)", i=GROUP_TILES) for out in (out_0, out_1)
    ]

    with ExitStack() as stack:
        stack.enter_context(tc.manual_schedule())
        keep = stack.enter_context(tc.tile_pool(name="keep", bufs=1))
        w_pool = stack.enter_context(tc.tile_pool(name="w", bufs=2))
        large_pool = stack.enter_context(tc.tile_pool(name="large", bufs=2 * BLOCKS))
        x_pool = stack.enter_context(tc.tile_pool(name="x", bufs=BLOCKS))
        stage = stack.enter_context(tc.tile_pool(name="stage", bufs=2))
        codes_pool = stack.enter_context(tc.tile_pool(name="codes", bufs=2 * PAIRS_IN_BLOCK + 1))
        small = stack.enter_context(tc.tile_pool(name="small", bufs=4))
        psum_x = stack.enter_context(tc.psum_pool(name="psum_x", bufs=PAIR))
        psum_y = stack.enter_context(tc.psum_pool(name="psum_y", bufs=3 * PAIR))

        w_raw = {}
        w_grouped = {}
        x_blocks = {}
        turned = {}
        grouped = {}
        quantised = {}
        sums = {}
        sum_sq = {}
        inv_rms = {}
        results = {}

        def load_weight(half):
            raw = large_pool.tile([P, PASSES, PACK, E], BF16, tag="large")
            for g in range(PASSES):
                nc.sync.dma_start(
                    out=raw[:, g, :, :],
                    in_=weights[half][g * K_PASS : (g + 1) * K_PASS, :].rearrange(
                        "(p t) n -> p t n", t=PACK
                    ),
                )
            w_raw[half] = raw

        def load_tokens(blk, first, end):
            if first == 0:
                x_sb = x_pool.tile([P, BLOCK_TILES, C], BF16)
                x_blocks[blk] = x_sb
            grp, start = divmod(blk * BLOCK_TILES, GROUP_TILES)
            nc.sync.dma_start(
                out=x_blocks[blk][:, first:end, :],
                in_=x_tiles[grp, :, start + first : start + end, :],
            )

        def regroup_weight(half, g, shares):
            side_by_side = w_pool.tile([P, E, PACK], BF16, align_bytes=64)
            for copy, first, end in shares:
                copy(
                    out=side_by_side[:, first:end, :].rearrange("p (c i) t -> p c t i", i=4),
                    in_=w_raw[half][:, g, :, first:end].rearrange("p t (c i) -> p c t i", i=4),
                )
            w_grouped[(half, g)] = side_by_side

        def quantise_weight(half, g):
            nc.vector.quantize_mx(
                out=w_codes[:, g, half, :].bitcast(FP8X4),
                scales=w_scales[:, g, half, :],
                in_=w_grouped[(half, g)][:].rearrange("p n t -> p (n t)"),
            )

        def turn(pair):
            blk, pr = divmod(pair, PAIRS_IN_BLOCK)
            banks = []
            for j in range(PAIR):
                words = x_blocks[blk][:, pr * PAIR + j, :].bitcast(F32)
                bank = psum_x.tile([P, PASSES * WORD_PLANES, P], F32)
                for c in range(PASSES * WORD_PLANES):
                    g, u = divmod(c, WORD_PLANES)
                    first = g * WORD_PLANES * P + u
                    nc.tensor.transpose(
                        bank[:, c, :],
                        words[:, first : (g + 1) * WORD_PLANES * P : WORD_PLANES],
                        ident[:],
                    )
                banks.append(bank)
            turned[pair] = banks
            side_by_side = stage.tile([P, PAIR, PASSES, P, PACK], BF16, align_bytes=64)
            grouped[pair] = side_by_side

        def regroup_tokens(pair, j, copy):
            copy(
                out=grouped[pair][:, j]
                .rearrange("p g r t -> p (g r t)")
                .bitcast(F32)
                .rearrange("p (g r u) -> p g r u", g=PASSES, u=WORD_PLANES),
                in_=turned[pair][j][:].rearrange("p (g u) r -> p g r u", u=WORD_PLANES),
            )

        def quantise_tokens(pair):
            x_codes = codes_pool.tile([P, PAIR, PASSES, P], U32, align_bytes=64)
            x_scales = codes_pool.tile([P, PAIR, PASSES, P], U8, align_bytes=64)
            nc.vector.quantize_mx(
                out=x_codes[:].rearrange("p j g r -> p (j g r)").bitcast(FP8X4),
                scales=x_scales[:].rearrange("p j g r -> p (j g r)"),
                in_=grouped[pair][:].rearrange("p j g r t -> p (j g r t)"),
            )
            quantised[pair] = (x_codes, x_scales)

        def place(unit):
            blk, rest = divmod(unit, UNITS_IN_BLOCK)
            if blk == BLOCKS - 1:
                pr, half = divmod(rest, 2)
            else:
                half, pr = divmod(rest, PAIRS_IN_BLOCK)
            return blk, half, pr

        def project(unit, order):
            blk, half, pr = place(unit)
            x_codes, x_scales = quantised[blk * PAIRS_IN_BLOCK + pr]
            banks = []
            for j in range(PAIR):
                y = psum_y.tile([P, E], F32)
                banks.append(y)
            for j, g in order:
                nc.tensor.matmul_mx(
                    out=banks[j][:],
                    lhsT=x_codes[:, j, g, :].bitcast(FP8X4),
                    lhsT_scale=x_scales[:, j, g, :],
                    rhs=w_codes[:, g, half, :].bitcast(FP8X4),
                    rhs_scale=w_scales[:, g, half, :],
                    start=(g == 0),
                    stop=(g == PASSES - 1),
                )
            sums[unit] = banks
            totals = small.tile([P, PAIR, H], F32)
            sum_sq[unit] = totals

        def sum_squares(unit, j):
            squares = small.tile([P, H, DH], BF16)
            for h in range(H):
                nc.scalar.activation(
                    out=squares[:, h, :],
                    in_=sums[unit][j][:, h * DH : (h + 1) * DH],
                    func=ACT.Square,
                    accum_out=sum_sq[unit][:, j, h : h + 1],
                )

        def inverse_rms(unit, first, end):
            factors = small.tile([P, PAIR, H], F32)
            nc.scalar.activation(
                out=factors[:, first:end, :],
                in_=sum_sq[unit][:, first:end, :],
                func=ACT.Abs_reciprocal_sqrt,
                scale=1.0 / DH,
                bias=eps[:, 0:1],
            )
            for j in range(first, end):
                inv_rms[(unit, j)] = factors

        def normalise(unit, j):
            blk, half, pr = place(unit)
            if pr == 0 and j == 0:
                res = large_pool.tile([P, H, BLOCK_TILES, DH], F32, tag="large")
                results[(blk, half)] = res
            nc.vector.tensor_tensor(
                out=results[(blk, half)][:, :, pr * PAIR + j, :],
                in0=sums[unit][j][:].rearrange("p (h d) -> p h d", h=H),
                in1=inv_rms[(unit, j)][:, j, :].unsqueeze(2).to_broadcast([P, H, DH]),
                op=ALU.mult,
            )

        def store(unit):
            blk, half, pr = place(unit)
            by_pair = blk >= BLOCKS - 2
            if by_pair or pr == PAIRS_IN_BLOCK - 1:
                first = pr * PAIR if by_pair else 0
                end = (pr + 1) * PAIR
                start = blk * BLOCK_TILES
                for r in range(RUNS):
                    nc.sync.dma_start(
                        out=out_runs[half][r, :, :, (start + first) * DH : (start + end) * DH],
                        in_=results[(blk, half)][r:P:RUNS, :, first:end, :].rearrange(
                            "p h i d -> p h (i d)"
                        ),
                    )

        load_tokens(0, 0, 1)
        load_tokens(0, 1, PAIR)
        load_weight(0)
        load_tokens(0, PAIR, BLOCK_TILES)
        load_weight(1)
        load_tokens(1, 0, PAIR)
        load_tokens(1, PAIR, BLOCK_TILES)
        for blk in range(2, BLOCKS):
            load_tokens(blk, 0, BLOCK_TILES)

        ident = keep.tile([P, P], F32)
        make_identity(nc, ident[:])
        eps = keep.tile([P, 1], F32)
        nc.vector.memset(eps[:], EPS)
        warm = keep.tile([P, 1], F32)
        nc.scalar.activation(out=warm[:], in_=eps[:], func=ACT.Abs_reciprocal_sqrt)
        w_codes = keep.tile([P, PASSES, 2, E], U32, align_bytes=64)
        w_scales = keep.tile([P, PASSES, 2, E], U8, align_bytes=64)

        TILE_BY_TILE = [(j, g) for j in range(PAIR) for g in range(PASSES)]
        PASS_BY_PASS = [(j, g) for g in range(PASSES) for j in range(PAIR)]
        VECTOR_ALONE = [(nc.vector.tensor_copy, 0, E)]
        MOSTLY_VECTOR = [(nc.scalar.copy, 3 * E // 4, E), (nc.vector.tensor_copy, 0, 3 * E // 4)]
        SHARED = [(nc.scalar.copy, E // 2, E), (nc.vector.tensor_copy, 0, E // 2)]

        turn(0)
        for j in range(PAIR):
            regroup_tokens(0, j, nc.scalar.copy)
        regroup_weight(0, 0, SHARED)
        quantise_tokens(0)
        regroup_weight(0, 1, SHARED)
        for g in range(PASSES):
            quantise_weight(0, g)
        turn(1)
        for j in range(PAIR):
            regroup_tokens(1, j, nc.scalar.copy)
        project(0, PASS_BY_PASS)
        regroup_weight(1, 0, MOSTLY_VECTOR)
        quantise_tokens(1)
        project(1, TILE_BY_TILE)
        regroup_weight(1, 1, VECTOR_ALONE)
        for g in range(PASSES):
            quantise_weight(1, g)
        sum_squares(0, 0)
        sum_squares(0, 1)
        turn(2)
        sum_squares(1, 0)
        inverse_rms(0, 0, PAIR)
        sum_squares(1, 1)
        regroup_tokens(2, 0, nc.scalar.copy)
        normalise(0, 0)
        regroup_tokens(2, 1, nc.vector.tensor_copy)
        normalise(0, 1)
        quantise_tokens(2)

        for u in range(2, UNITS):
            even = u % 2 == 0
            ahead = u // 2 + PAIRS_AHEAD
            prepare = ahead < PAIRS
            project(u, TILE_BY_TILE)
            if even and prepare:
                turn(ahead)
            sum_squares(u, 0)
            inverse_rms(u - 1, 0, PAIR)
            if u == UNITS - 1:
                inverse_rms(u, 0, 1)
            sum_squares(u, 1)
            if even and prepare:
                regroup_tokens(ahead, 0, nc.scalar.copy)
            normalise(u - 1, 0)
            if prepare and not even:
                quantise_tokens(ahead)
            normalise(u - 1, 1)
            if prepare and even:
                regroup_tokens(ahead, 1, nc.vector.tensor_copy)
            store(u - 1)
        normalise(UNITS - 1, 0)
        inverse_rms(UNITS - 1, 1, PAIR)
        normalise(UNITS - 1, 1)
        store(UNITS - 1)
